import numpy as np
import ml_dtypes


def mxq(x, axis, fmt="e4m3"):
    dtype, down = {"e4m3": (ml_dtypes.float8_e4m3fn, 7), "e5m2": (ml_dtypes.float8_e5m2, 14)}[fmt]
    v = np.moveaxis(np.asarray(x, np.float32).astype(ml_dtypes.bfloat16).astype(np.float64), axis, -1)
    blocks = v.reshape(v.shape[:-1] + (-1, 32))
    amax = np.abs(blocks).max(-1, keepdims=True)
    byte = np.maximum(np.where(amax > 0, np.frexp(amax)[1] - 1 + 127, 0) - down, 1)
    scale = np.exp2(byte - 127.0)
    codes = (blocks / scale).astype(np.float32).astype(dtype).astype(np.float64)
    return np.moveaxis((codes * scale).reshape(v.shape), -1, axis)


WIDE = False


def mx_kscale(k):
    if not WIDE:
        return np.ones(k)
    levels = np.array([10, -10, 5, -5, 0])
    a = np.random.permutation(np.resize(levels, k // 512 * 4)).reshape(k // 512, 4)
    idx = np.arange(k)
    return np.exp2(a[idx // 512, idx % 128 // 32])


BF16 = ml_dtypes.bfloat16


def bf(x):
    return np.asarray(x, np.float32).astype(BF16)


def f64(x):
    return np.asarray(x).astype(np.float64)


B, S, K, H, D = 4, 384, 128, 1024, 1024
EPS = 1e-6


def setup_inputs():
    s = mx_kscale(H)
    rows = 0.5 * np.exp(0.5 * np.random.standard_normal((B, S, 1)))
    return {"hidden_states": bf(np.random.standard_normal((B, S, H)) * rows),
            "memory_state": bf(np.random.standard_normal((B, K, H)) * s),
            "q_w": bf(np.random.standard_normal((D, H)) * 1.5 / np.sqrt(H) / s),
            "k_w": bf(np.random.standard_normal((D, H)) * 1.5 / np.sqrt(H) / s),
            "norm_w": bf((1.0 + 0.3 * np.random.standard_normal(H)) * s)}


def reference(hidden_states, memory_state, q_w, k_w, norm_w):
    x = f64(hidden_states)
    normed = x * (1.0 / np.sqrt(np.mean(x * x, axis=-1, keepdims=True) + EPS)) * f64(norm_w)
    pool = np.concatenate([normed, f64(memory_state)], axis=1)
    pq = mxq(pool, 2, "e4m3")
    q = pq[:, :S] @ mxq(f64(q_w), 1, "e4m3").T
    k = pq @ mxq(f64(k_w), 1, "e4m3").T
    return q, k

@@ -1,0 +1,236 @@
+from contextlib import ExitStack
+
+import concourse.masks as masks
+import concourse.mybir as mybir
+
+F32 = mybir.dt.float32
+BF16 = mybir.dt.bfloat16
+I32 = mybir.dt.int32
+U32 = mybir.dt.uint32
+U8 = mybir.dt.uint8
+FP8X4 = mybir.dt.float8_e4m3fn_x4
+ACT = mybir.ActivationFunctionType
+ALU = mybir.AluOpType
+
+P = 128
+PACK = 4
+PAIR = 2
+BATCHES, TOKENS, MEMORY, H, D = 4, 384, 128, 1024, 1024
+EPS = 1e-6
+PASSES = H // (P * PACK)
+HALVES = PACK // PAIR
+TOKEN_TILES = TOKENS // P
+N_TILE = 512
+ROW_BLOCKS = N_TILE // P
+COLUMN_TILES = D // N_TILE
+
+FLOPS = 2 * H * D * BATCHES * (TOKENS + TOKENS + MEMORY)
+
+
+def tile_memresprojections_pa_kernel(
+    tc, hidden_states, memory_state, q_w, k_w, norm_w, out_0, out_1
+):
+    nc = tc.nc
+    with ExitStack() as ctx:
+        const = ctx.enter_context(tc.tile_pool(name="const", bufs=1))
+        inputs = ctx.enter_context(tc.tile_pool(name="inputs", bufs=1))
+        operands = ctx.enter_context(tc.tile_pool(name="operands", bufs=1))
+        stage = ctx.enter_context(tc.tile_pool(name="stage", bufs=3))
+        results = ctx.enter_context(tc.tile_pool(name="results", bufs=6))
+        turned_banks = ctx.enter_context(tc.psum_pool(name="turned_banks", bufs=4))
+        sum_banks = ctx.enter_context(tc.psum_pool(name="sum_banks", bufs=4))
+
+        gain_row = const.tile([P, H], BF16)
+        nc.vector.memset(gain_row[:].bitcast(I32), 0)
+        nc.sync.dma_start(out=gain_row[0:1, :], in_=norm_w.unsqueeze(0))
+
+        def load_tokens(b):
+            loaded = inputs.tile([P, TOKEN_TILES, H], BF16, name="tokens%d" % b)
+            nc.sync.dma_start(
+                out=loaded[:],
+                in_=hidden_states[b].rearrange("(p i) h -> p i h", i=TOKEN_TILES),
+            )
+            return loaded
+
+        def load_rows(source, label):
+            rows = inputs.tile([P, ROW_BLOCKS, H], BF16, name=label)
+            nc.sync.dma_start(out=rows[:], in_=source.rearrange("(j p) h -> p j h", p=P))
+            return rows
+
+        tokens = [load_tokens(0)]
+        q_rows = [load_rows(q_w[c * N_TILE : (c + 1) * N_TILE, :], "q_rows%d" % c) for c in range(COLUMN_TILES)]
+        tokens.append(load_tokens(1))
+        k_rows = [load_rows(k_w[c * N_TILE : (c + 1) * N_TILE, :], "k_rows%d" % c) for c in range(COLUMN_TILES)]
+        memory_rows = load_rows(memory_state.flatten_outer_dims(), "memory_rows")
+        tokens.append(load_tokens(2))
+        tokens.append(load_tokens(3))
+
+        eps = const.tile([P, 1], F32)
+        nc.vector.memset(eps[:], EPS)
+        table_warmer = const.tile([P, 1], F32)
+        nc.scalar.activation(out=table_warmer[:], in_=eps[:], func=ACT.Sqrt)
+        ident_f32 = const.tile([P, P], F32)
+        masks.make_identity(nc, ident_f32[:])
+        ident_bf16 = const.tile([P, P], BF16)
+        masks.make_identity(nc, ident_bf16[:])
+        ones = const.tile([P, P], BF16)
+        nc.vector.memset(ones[:], 1.0)
+
+        gain = const.tile([P, PAIR, H // PAIR], BF16)
+        for c in range(H // N_TILE):
+            spread = sum_banks.tile([P, N_TILE], F32, tag="sums")
+            nc.tensor.matmul(
+                spread[:], lhsT=ones[:], rhs=gain_row[:, c * N_TILE : (c + 1) * N_TILE],
+                start=True, stop=True,
+            )
+            pairs = N_TILE // PAIR
+            nc.vector.tensor_copy(
+                out=gain[:, :, c * pairs : (c + 1) * pairs],
+                in_=spread[:].rearrange("p (w e) -> p e w", e=PAIR),
+            )
+
+        mean_sq = [const.tile([P, TOKEN_TILES], F32, name="mean_sq%d" % b) for b in range(BATCHES)]
+        rms = [const.tile([P, TOKEN_TILES], F32, name="rms%d" % b) for b in range(BATCHES)]
+        inv_rms = [const.tile([P, TOKEN_TILES], F32, name="inv_rms%d" % b) for b in range(BATCHES)]
+        normed = {}
+        turned = {}
+        pool_mx = {}
+
+        def mean_square(b, i):
+            squares = stage.tile([P, H], BF16, tag="squares")
+            nc.scalar.activation(
+                out=squares[:], in_=tokens[b][:, i, :], func=ACT.Square,
+                scale=H**-0.5, accum_out=mean_sq[b][:, i : i + 1],
+            )
+
+        def inverse_rms(b):
+            nc.scalar.activation(out=rms[b][:], in_=mean_sq[b][:], func=ACT.Sqrt, bias=eps[:])
+            nc.vector.reciprocal(out=inv_rms[b][:], in_=rms[b][:])
+
+        def apply_norm(b, i):
+            n = stage.tile([P, PAIR, H // PAIR], BF16, tag="normed", bufs=2 * TOKEN_TILES, name="n%d_%d" % (b, i))
+            nc.vector.scalar_tensor_tensor(
+                out=n[:],
+                in0=tokens[b][:, i, :].rearrange("p (w e) -> p e w", e=PAIR),
+                scalar=inv_rms[b][:, i : i + 1],
+                in1=gain[:],
+                op0=ALU.mult,
+                op1=ALU.mult,
+            )
+            normed[b, i] = n
+
+        def turn_normed(b, i):
+            bank = turned_banks.tile([P, PASSES, PACK, P], BF16, tag="turned", name="turned%d_%d" % (b, i))
+            for g in range(PASSES):
+                for u in range(HALVES):
+                    first = (HALVES * g + u) * P
+                    for e in range(PAIR):
+                        nc.tensor.transpose(
+                            bank[:, g, PAIR * u + e, :], normed[b, i][:, e, first : first + P], ident_bf16[:]
+                        )
+            turned[b, i] = bank
+
+        def quantise_normed(b, i):
+            grouped = stage.tile([P, PASSES, P, PACK], BF16, tag="grouped_tokens", align_bytes=64)
+            nc.scalar.copy(out=grouped[:], in_=turned[b, i][:].rearrange("p g t r -> p g r t"))
+            codes = operands.tile([P, PASSES, P], U32, name="codes%d_%d" % (b, i), align_bytes=64)
+            scales = operands.tile([P, PASSES, P], U8, name="scales%d_%d" % (b, i), align_bytes=64)
+            nc.vector.quantize_mx(
+                out=codes[:].rearrange("p g r -> p (g r)").bitcast(FP8X4),
+                scales=scales[:].rearrange("p g r -> p (g r)"),
+                in_=grouped[:].rearrange("p g r t -> p (g r t)"),
+            )
+            pool_mx[b, i] = (codes, scales)
+
+        def quantise_rows(rows, label):
+            grouped = stage.tile([P, PASSES * N_TILE * PACK], BF16, tag="grouped_rows", bufs=2, align_bytes=64)
+            grouped_words = grouped[:].bitcast(F32).rearrange("p (g r u) -> p g r u", g=PASSES, u=HALVES)
+            for j in range(ROW_BLOCKS):
+                words = rows[:, j, :].bitcast(F32)
+                bank = turned_banks.tile([P, PASSES, HALVES, P], F32, tag="turned")
+                for g in range(PASSES):
+                    for u in range(HALVES):
+                        first = (HALVES * g + u) * P
+                        nc.tensor.transpose(bank[:, g, u, :], words[:, first : first + P], ident_f32[:])
+                copy = nc.scalar.copy if j % 2 == 0 else nc.vector.tensor_copy
+                copy(
+                    out=grouped_words[:, :, j * P : (j + 1) * P, :],
+                    in_=bank[:].rearrange("p g u r -> p g r u"),
+                )
+            codes = operands.tile([P, PASSES, N_TILE], U32, name=label + "_codes", align_bytes=64)
+            scales = operands.tile([P, PASSES, N_TILE], U8, name=label + "_scales", align_bytes=64)
+            width = N_TILE * PACK
+            for g in range(PASSES):
+                nc.vector.quantize_mx(
+                    out=codes[:, g, :].bitcast(FP8X4),
+                    scales=scales[:, g, :],
+                    in_=grouped[:, g * width : (g + 1) * width],
+                )
+            return codes, scales
+
+        def project(token_mx, token_columns, weight_mx, copies, out_rows):
+            token_codes, token_scales = token_mx
+            result = results.tile([P, D], F32, tag="result")
+            for c in range(COLUMN_TILES):
+                weight_codes, weight_scales = weight_mx[c]
+                sums = sum_banks.tile([P, N_TILE], F32, tag="sums")
+                for g in range(PASSES):
+                    nc.tensor.matmul_mx(
+                        out=sums[:],
+                        lhsT=token_codes[:, g, token_columns].bitcast(FP8X4),
+                        lhsT_scale=token_scales[:, g, token_columns],
+                        rhs=weight_codes[:, g, :].bitcast(FP8X4),
+                        rhs_scale=weight_scales[:, g, :],
+                        start=(g == 0),
+                        stop=(g == PASSES - 1),
+                    )
+                copies[c](out=result[:, c * N_TILE : (c + 1) * N_TILE], in_=sums[:])
+            nc.sync.dma_start(out=out_rows, in_=result[:])
+
+        all_columns = slice(0, P)
+        q_copies = [nc.vector.tensor_copy, nc.vector.tensor_copy]
+        k_copies = [nc.scalar.copy, nc.vector.tensor_copy]
+
+        def q_part(b):
+            q_tiles = out_0[b].rearrange("(p i) d -> p i d", i=TOKEN_TILES)
+            for i in range(TOKEN_TILES):
+                project(pool_mx[b, i], all_columns, q_mx, q_copies, q_tiles[:, i, :])
+                if b + 2 < BATCHES:
+                    mean_square(b + 2, i)
+            if b + 2 < BATCHES:
+                inverse_rms(b + 2)
+
+        def k_part(b):
+            if b + 1 < BATCHES:
+                for i in range(TOKEN_TILES):
+                    turn_normed(b + 1, i)
+            k_tiles = out_1[b, 0:TOKENS, :].rearrange("(p i) d -> p i d", i=TOKEN_TILES)
+            for i in range(TOKEN_TILES):
+                project(pool_mx[b, i], all_columns, k_mx, k_copies, k_tiles[:, i, :])
+                if b + 1 < BATCHES:
+                    quantise_normed(b + 1, i)
+                if b + 2 < BATCHES:
+                    apply_norm(b + 2, i)
+            project(memory_mx, slice(b * P, (b + 1) * P), k_mx, k_copies, out_1[b, TOKENS : TOKENS + MEMORY, :])
+
+        def norm_batch(b):
+            for i in range(TOKEN_TILES):
+                mean_square(b, i)
+            inverse_rms(b)
+            for i in range(TOKEN_TILES):
+                apply_norm(b, i)
+
+        norm_batch(0)
+        q_mx = [quantise_rows(q_rows[c], "q%d" % c) for c in range(COLUMN_TILES)]
+        for i in range(TOKEN_TILES):
+            turn_normed(0, i)
+        for i in range(TOKEN_TILES):
+            quantise_normed(0, i)
+        norm_batch(1)
+        q_part(0)
+        k_mx = [quantise_rows(k_rows[c], "k%d" % c) for c in range(COLUMN_TILES)]
+        memory_mx = quantise_rows(memory_rows, "memory")
+        k_part(0)
+        for b in range(1, BATCHES):
+            q_part(b)
+            k_part(b)

@@ -19,10 +19,13 @@ BATCHES, TOKENS, MEMORY, H, D = 4, 384, 128, 1024, 1024
 EPS = 1e-6
 PASSES = H // (P * PACK)
 HALVES = PACK // PAIR
-TOKEN_TILES = TOKENS // P
+BATCH_TILES = TOKENS // P
+TILES = BATCHES * BATCH_TILES
 N_TILE = 512
 ROW_BLOCKS = N_TILE // P
 COLUMN_TILES = D // N_TILE
+NORM_AHEAD = 3
+TURN_AHEAD = 1
 
 FLOPS = 2 * H * D * BATCHES * (TOKENS + TOKENS + MEMORY)
 
@@ -32,130 +35,163 @@ def tile_memresprojections_pa_kernel(
 ):
     nc = tc.nc
     with ExitStack() as ctx:
+        ctx.enter_context(tc.manual_schedule())
         const = ctx.enter_context(tc.tile_pool(name="const", bufs=1))
         inputs = ctx.enter_context(tc.tile_pool(name="inputs", bufs=1))
         operands = ctx.enter_context(tc.tile_pool(name="operands", bufs=1))
-        stage = ctx.enter_context(tc.tile_pool(name="stage", bufs=3))
-        results = ctx.enter_context(tc.tile_pool(name="results", bufs=6))
-        turned_banks = ctx.enter_context(tc.psum_pool(name="turned_banks", bufs=4))
-        sum_banks = ctx.enter_context(tc.psum_pool(name="sum_banks", bufs=4))
+        stage = ctx.enter_context(tc.tile_pool(name="stage", bufs=4))
+        results = ctx.enter_context(tc.tile_pool(name="results", bufs=8))
+        banks = ctx.enter_context(tc.psum_pool(name="banks", bufs=8))
 
         gain_row = const.tile([P, H], BF16)
         nc.vector.memset(gain_row[:].bitcast(I32), 0)
         nc.sync.dma_start(out=gain_row[0:1, :], in_=norm_w.unsqueeze(0))
 
-        def load_tokens(b):
-            loaded = inputs.tile([P, TOKEN_TILES, H], BF16, name="tokens%d" % b)
-            nc.sync.dma_start(
-                out=loaded[:],
-                in_=hidden_states[b].rearrange("(p i) h -> p i h", i=TOKEN_TILES),
-            )
-            return loaded
+        token_rows = hidden_states.flatten_outer_dims()
+        tokens = {}
+
+        def load_tokens(n):
+            tokens[n] = inputs.tile([P, H], BF16, name="tokens%d" % n)
+            nc.sync.dma_start(out=tokens[n][:], in_=token_rows[n * P : (n + 1) * P, :])
 
         def load_rows(source, label):
             rows = inputs.tile([P, ROW_BLOCKS, H], BF16, name=label)
             nc.sync.dma_start(out=rows[:], in_=source.rearrange("(j p) h -> p j h", p=P))
             return rows
 
-        tokens = [load_tokens(0)]
-        q_rows = [load_rows(q_w[c * N_TILE : (c + 1) * N_TILE, :], "q_rows%d" % c) for c in range(COLUMN_TILES)]
-        tokens.append(load_tokens(1))
-        k_rows = [load_rows(k_w[c * N_TILE : (c + 1) * N_TILE, :], "k_rows%d" % c) for c in range(COLUMN_TILES)]
+        load_tokens(0)
+        q_rows0 = load_rows(q_w[0:N_TILE, :], "q_rows0")
+        load_tokens(1)
+        q_rows1 = load_rows(q_w[N_TILE:D, :], "q_rows1")
+        load_tokens(2)
+        k_rows0 = load_rows(k_w[0:N_TILE, :], "k_rows0")
+        k_rows1 = load_rows(k_w[N_TILE:D, :], "k_rows1")
+        load_tokens(3)
         memory_rows = load_rows(memory_state.flatten_outer_dims(), "memory_rows")
-        tokens.append(load_tokens(2))
-        tokens.append(load_tokens(3))
+        for n in range(4, TILES):
+            load_tokens(n)
 
         eps = const.tile([P, 1], F32)
         nc.vector.memset(eps[:], EPS)
         table_warmer = const.tile([P, 1], F32)
         nc.scalar.activation(out=table_warmer[:], in_=eps[:], func=ACT.Sqrt)
+        ones = const.tile([P, P], BF16)
+        nc.vector.memset(ones[:], 1.0)
         ident_f32 = const.tile([P, P], F32)
         masks.make_identity(nc, ident_f32[:])
         ident_bf16 = const.tile([P, P], BF16)
         masks.make_identity(nc, ident_bf16[:])
-        ones = const.tile([P, P], BF16)
-        nc.vector.memset(ones[:], 1.0)
 
         gain = const.tile([P, PAIR, H // PAIR], BF16)
+        pairs = N_TILE // PAIR
         for c in range(H // N_TILE):
-            spread = sum_banks.tile([P, N_TILE], F32, tag="sums")
+            spread = banks.tile([P, N_TILE], F32, tag="bank")
             nc.tensor.matmul(
                 spread[:], lhsT=ones[:], rhs=gain_row[:, c * N_TILE : (c + 1) * N_TILE],
                 start=True, stop=True,
             )
-            pairs = N_TILE // PAIR
             nc.vector.tensor_copy(
                 out=gain[:, :, c * pairs : (c + 1) * pairs],
                 in_=spread[:].rearrange("p (w e) -> p e w", e=PAIR),
             )
 
-        mean_sq = [const.tile([P, TOKEN_TILES], F32, name="mean_sq%d" % b) for b in range(BATCHES)]
-        rms = [const.tile([P, TOKEN_TILES], F32, name="rms%d" % b) for b in range(BATCHES)]
-        inv_rms = [const.tile([P, TOKEN_TILES], F32, name="inv_rms%d" % b) for b in range(BATCHES)]
+        inv_rms = {}
         normed = {}
         turned = {}
+        grouped = {}
         pool_mx = {}
 
-        def mean_square(b, i):
+        def mean_square(n):
             squares = stage.tile([P, H], BF16, tag="squares")
+            mean_sq = stage.tile([P, 1], F32, tag="mean_sq")
             nc.scalar.activation(
-                out=squares[:], in_=tokens[b][:, i, :], func=ACT.Square,
-                scale=H**-0.5, accum_out=mean_sq[b][:, i : i + 1],
+                out=squares[:], in_=tokens[n][:], func=ACT.Square, scale=H**-0.5, accum_out=mean_sq[:]
             )
+            rms = stage.tile([P, 1], F32, tag="rms")
+            nc.scalar.activation(out=rms[:], in_=mean_sq[:], func=ACT.Sqrt, bias=eps[:])
+            inv_rms[n] = stage.tile([P, 1], F32, tag="inv_rms", name="inv_rms%d" % n)
+            nc.vector.reciprocal(out=inv_rms[n][:], in_=rms[:])
 
-        def inverse_rms(b):
-            nc.scalar.activation(out=rms[b][:], in_=mean_sq[b][:], func=ACT.Sqrt, bias=eps[:])
-            nc.vector.reciprocal(out=inv_rms[b][:], in_=rms[b][:])
-
-        def apply_norm(b, i):
-            n = stage.tile([P, PAIR, H // PAIR], BF16, tag="normed", bufs=2 * TOKEN_TILES, name="n%d_%d" % (b, i))
+        def norm(n):
+            normed[n] = stage.tile([P, PAIR, H // PAIR], BF16, tag="normed", name="normed%d" % n)
             nc.vector.scalar_tensor_tensor(
-                out=n[:],
-                in0=tokens[b][:, i, :].rearrange("p (w e) -> p e w", e=PAIR),
-                scalar=inv_rms[b][:, i : i + 1],
+                out=normed[n][:],
+                in0=tokens[n][:].rearrange("p (w e) -> p e w", e=PAIR),
+                scalar=inv_rms[n][:],
                 in1=gain[:],
                 op0=ALU.mult,
                 op1=ALU.mult,
             )
-            normed[b, i] = n
 
-        def turn_normed(b, i):
-            bank = turned_banks.tile([P, PASSES, PACK, P], BF16, tag="turned", name="turned%d_%d" % (b, i))
+        def turn(n):
+            turned[n] = banks.tile([P, PASSES, PACK, P], BF16, tag="bank", name="turned%d" % n)
             for g in range(PASSES):
                 for u in range(HALVES):
                     first = (HALVES * g + u) * P
                     for e in range(PAIR):
                         nc.tensor.transpose(
-                            bank[:, g, PAIR * u + e, :], normed[b, i][:, e, first : first + P], ident_bf16[:]
+                            turned[n][:, g, PAIR * u + e, :], normed[n][:, e, first : first + P], ident_bf16[:]
                         )
-            turned[b, i] = bank
 
-        def quantise_normed(b, i):
-            grouped = stage.tile([P, PASSES, P, PACK], BF16, tag="grouped_tokens", align_bytes=64)
-            nc.scalar.copy(out=grouped[:], in_=turned[b, i][:].rearrange("p g t r -> p g r t"))
-            codes = operands.tile([P, PASSES, P], U32, name="codes%d_%d" % (b, i), align_bytes=64)
-            scales = operands.tile([P, PASSES, P], U8, name="scales%d_%d" % (b, i), align_bytes=64)
+        def group(n):
+            grouped[n] = stage.tile(
+                [P, PASSES, P, PACK], BF16, tag="grouped", name="grouped%d" % n, align_bytes=64
+            )
+            nc.scalar.copy(out=grouped[n][:], in_=turned[n][:].rearrange("p g t r -> p g r t"))
+
+        def quantise(n):
+            codes = operands.tile([P, PASSES, P], U32, name="codes%d" % n, align_bytes=64)
+            scales = operands.tile([P, PASSES, P], U8, name="scales%d" % n, align_bytes=64)
             nc.vector.quantize_mx(
                 out=codes[:].rearrange("p g r -> p (g r)").bitcast(FP8X4),
                 scales=scales[:].rearrange("p g r -> p (g r)"),
-                in_=grouped[:].rearrange("p g r t -> p (g r t)"),
+                in_=grouped[n][:].rearrange("p g r t -> p (g r t)"),
             )
-            pool_mx[b, i] = (codes, scales)
+            pool_mx[n] = (codes, scales)
+
+        def matmuls(token_mx, token_columns, weight_mx):
+            token_codes, token_scales = token_mx
+            sums = []
+            for weight_codes, weight_scales in weight_mx:
+                bank = banks.tile([P, N_TILE], F32, tag="bank")
+                for g in range(PASSES):
+                    nc.tensor.matmul_mx(
+                        out=bank[:],
+                        lhsT=token_codes[:, g, token_columns].bitcast(FP8X4),
+                        lhsT_scale=token_scales[:, g, token_columns],
+                        rhs=weight_codes[:, g, :].bitcast(FP8X4),
+                        rhs_scale=weight_scales[:, g, :],
+                        start=(g == 0),
+                        stop=(g == PASSES - 1),
+                    )
+                sums.append(bank)
+            return sums
+
+        def store(sums, copies, out_rows):
+            result = results.tile([P, D], F32, tag="result")
+            for c in range(COLUMN_TILES):
+                copies[c](out=result[:, c * N_TILE : (c + 1) * N_TILE], in_=sums[c][:])
+            nc.sync.dma_start(out=out_rows, in_=result[:])
 
         def quantise_rows(rows, label):
-            grouped = stage.tile([P, PASSES * N_TILE * PACK], BF16, tag="grouped_rows", bufs=2, align_bytes=64)
-            grouped_words = grouped[:].bitcast(F32).rearrange("p (g r u) -> p g r u", g=PASSES, u=HALVES)
+            side_by_side = stage.tile(
+                [P, PASSES * N_TILE * PACK], BF16, tag="side_by_side", bufs=2, align_bytes=64
+            )
+            as_words = side_by_side[:].bitcast(F32).rearrange("p (g r u) -> p g r u", g=PASSES, u=HALVES)
+            row_banks = []
             for j in range(ROW_BLOCKS):
                 words = rows[:, j, :].bitcast(F32)
-                bank = turned_banks.tile([P, PASSES, HALVES, P], F32, tag="turned")
+                bank = banks.tile([P, PASSES, HALVES, P], F32, tag="bank")
                 for g in range(PASSES):
                     for u in range(HALVES):
                         first = (HALVES * g + u) * P
                         nc.tensor.transpose(bank[:, g, u, :], words[:, first : first + P], ident_f32[:])
-                copy = nc.scalar.copy if j % 2 == 0 else nc.vector.tensor_copy
+                row_banks.append(bank)
+            for j in range(ROW_BLOCKS):
+                copy = nc.vector.tensor_copy if j == ROW_BLOCKS - 1 else nc.scalar.copy
                 copy(
-                    out=grouped_words[:, :, j * P : (j + 1) * P, :],
-                    in_=bank[:].rearrange("p g u r -> p g r u"),
+                    out=as_words[:, :, j * P : (j + 1) * P, :],
+                    in_=row_banks[j][:].rearrange("p g u r -> p g r u"),
                 )
             codes = operands.tile([P, PASSES, N_TILE], U32, name=label + "_codes", align_bytes=64)
             scales = operands.tile([P, PASSES, N_TILE], U8, name=label + "_scales", align_bytes=64)
@@ -164,73 +200,46 @@ def tile_memresprojections_pa_kernel(
                 nc.vector.quantize_mx(
                     out=codes[:, g, :].bitcast(FP8X4),
                     scales=scales[:, g, :],
-                    in_=grouped[:, g * width : (g + 1) * width],
+                    in_=side_by_side[:, g * width : (g + 1) * width],
                 )
             return codes, scales
 
-        def project(token_mx, token_columns, weight_mx, copies, out_rows):
-            token_codes, token_scales = token_mx
-            result = results.tile([P, D], F32, tag="result")
-            for c in range(COLUMN_TILES):
-                weight_codes, weight_scales = weight_mx[c]
-                sums = sum_banks.tile([P, N_TILE], F32, tag="sums")
-                for g in range(PASSES):
-                    nc.tensor.matmul_mx(
-                        out=sums[:],
-                        lhsT=token_codes[:, g, token_columns].bitcast(FP8X4),
-                        lhsT_scale=token_scales[:, g, token_columns],
-                        rhs=weight_codes[:, g, :].bitcast(FP8X4),
-                        rhs_scale=weight_scales[:, g, :],
-                        start=(g == 0),
-                        stop=(g == PASSES - 1),
-                    )
-                copies[c](out=result[:, c * N_TILE : (c + 1) * N_TILE], in_=sums[:])
-            nc.sync.dma_start(out=out_rows, in_=result[:])
+        mean_square(0)
+        norm(0)
+        q_mx = [quantise_rows(q_rows0, "q0")]
+        turn(0)
+        group(0)
+        quantise(0)
+        mean_square(1)
+        norm(1)
+        q_mx.append(quantise_rows(q_rows1, "q1"))
+        mean_square(2)
+        norm(2)
+        k_mx = [quantise_rows(k_rows0, "k0"), quantise_rows(k_rows1, "k1")]
 
+        q_copies = [nc.scalar.copy, nc.vector.tensor_copy]
+        k_copies = [nc.vector.tensor_copy, nc.vector.tensor_copy]
+        memory_copies = [nc.scalar.copy, nc.scalar.copy]
+
+        q_out = out_0.flatten_outer_dims()
         all_columns = slice(0, P)
-        q_copies = [nc.vector.tensor_copy, nc.vector.tensor_copy]
-        k_copies = [nc.scalar.copy, nc.vector.tensor_copy]
-
-        def q_part(b):
-            q_tiles = out_0[b].rearrange("(p i) d -> p i d", i=TOKEN_TILES)
-            for i in range(TOKEN_TILES):
-                project(pool_mx[b, i], all_columns, q_mx, q_copies, q_tiles[:, i, :])
-                if b + 2 < BATCHES:
-                    mean_square(b + 2, i)
-            if b + 2 < BATCHES:
-                inverse_rms(b + 2)
-
-        def k_part(b):
-            if b + 1 < BATCHES:
-                for i in range(TOKEN_TILES):
-                    turn_normed(b + 1, i)
-            k_tiles = out_1[b, 0:TOKENS, :].rearrange("(p i) d -> p i d", i=TOKEN_TILES)
-            for i in range(TOKEN_TILES):
-                project(pool_mx[b, i], all_columns, k_mx, k_copies, k_tiles[:, i, :])
-                if b + 1 < BATCHES:
-                    quantise_normed(b + 1, i)
-                if b + 2 < BATCHES:
-                    apply_norm(b + 2, i)
-            project(memory_mx, slice(b * P, (b + 1) * P), k_mx, k_copies, out_1[b, TOKENS : TOKENS + MEMORY, :])
-
-        def norm_batch(b):
-            for i in range(TOKEN_TILES):
-                mean_square(b, i)
-            inverse_rms(b)
-            for i in range(TOKEN_TILES):
-                apply_norm(b, i)
-
-        norm_batch(0)
-        q_mx = [quantise_rows(q_rows[c], "q%d" % c) for c in range(COLUMN_TILES)]
-        for i in range(TOKEN_TILES):
-            turn_normed(0, i)
-        for i in range(TOKEN_TILES):
-            quantise_normed(0, i)
-        norm_batch(1)
-        q_part(0)
-        k_mx = [quantise_rows(k_rows[c], "k%d" % c) for c in range(COLUMN_TILES)]
-        memory_mx = quantise_rows(memory_rows, "memory")
-        k_part(0)
-        for b in range(1, BATCHES):
-            q_part(b)
-            k_part(b)
+        for n in range(TILES):
+            b, i = divmod(n, BATCH_TILES)
+            if n + TURN_AHEAD < TILES:
+                turn(n + TURN_AHEAD)
+            q_sums = matmuls(pool_mx[n], all_columns, q_mx)
+            k_sums = matmuls(pool_mx[n], all_columns, k_mx)
+            if n + TURN_AHEAD < TILES:
+                group(n + TURN_AHEAD)
+            store(q_sums, q_copies, q_out[n * P : (n + 1) * P, :])
+            if n + TURN_AHEAD < TILES:
+                quantise(n + TURN_AHEAD)
+            store(k_sums, k_copies, out_1[b, i * P : (i + 1) * P, :])
+            if n + NORM_AHEAD < TILES:
+                mean_square(n + NORM_AHEAD)
+                norm(n + NORM_AHEAD)
+            if n == 0:
+                memory_mx = quantise_rows(memory_rows, "memory")
+            if i == BATCH_TILES - 1:
+                memory_sums = matmuls(memory_mx, slice(b * P, (b + 1) * P), k_mx)
+                store(memory_sums, memory_copies, out_1[b, TOKENS : TOKENS + MEMORY, :])

@@ -35,7 +35,6 @@ def tile_memresprojections_pa_kernel(
 ):
     nc = tc.nc
     with ExitStack() as ctx:
-        ctx.enter_context(tc.manual_schedule())
         const = ctx.enter_context(tc.tile_pool(name="const", bufs=1))
         inputs = ctx.enter_context(tc.tile_pool(name="inputs", bufs=1))
         operands = ctx.enter_context(tc.tile_pool(name="operands", bufs=1))

@@ -24,6 +24,7 @@ TILES = BATCHES * BATCH_TILES
 N_TILE = 512
 ROW_BLOCKS = N_TILE // P
 COLUMN_TILES = D // N_TILE
+SQUARE_AHEAD = 4
 NORM_AHEAD = 3
 TURN_AHEAD = 1
 
@@ -35,6 +36,7 @@ def tile_memresprojections_pa_kernel(
 ):
     nc = tc.nc
     with ExitStack() as ctx:
+        ctx.enter_context(tc.manual_schedule())
         const = ctx.enter_context(tc.tile_pool(name="const", bufs=1))
         inputs = ctx.enter_context(tc.tile_pool(name="inputs", bufs=1))
         operands = ctx.enter_context(tc.tile_pool(name="operands", bufs=1))
@@ -58,22 +60,21 @@ def tile_memresprojections_pa_kernel(
             nc.sync.dma_start(out=rows[:], in_=source.rearrange("(j p) h -> p j h", p=P))
             return rows
 
-        load_tokens(0)
+        for n in range(NORM_AHEAD):
+            load_tokens(n)
         q_rows0 = load_rows(q_w[0:N_TILE, :], "q_rows0")
-        load_tokens(1)
         q_rows1 = load_rows(q_w[N_TILE:D, :], "q_rows1")
-        load_tokens(2)
         k_rows0 = load_rows(k_w[0:N_TILE, :], "k_rows0")
         k_rows1 = load_rows(k_w[N_TILE:D, :], "k_rows1")
-        load_tokens(3)
+        load_tokens(NORM_AHEAD)
         memory_rows = load_rows(memory_state.flatten_outer_dims(), "memory_rows")
-        for n in range(4, TILES):
+        for n in range(NORM_AHEAD + 1, TILES):
             load_tokens(n)
 
-        eps = const.tile([P, 1], F32)
-        nc.vector.memset(eps[:], EPS)
+        minus_half = const.tile([P, 1], F32)
+        nc.vector.memset(minus_half[:], -0.5)
         table_warmer = const.tile([P, 1], F32)
-        nc.scalar.activation(out=table_warmer[:], in_=eps[:], func=ACT.Sqrt)
+        nc.scalar.activation(out=table_warmer[:], in_=minus_half[:], func=ACT.Square)
         ones = const.tile([P, P], BF16)
         nc.vector.memset(ones[:], 1.0)
         ident_f32 = const.tile([P, P], F32)
@@ -106,10 +107,12 @@ def tile_memresprojections_pa_kernel(
             nc.scalar.activation(
                 out=squares[:], in_=tokens[n][:], func=ACT.Square, scale=H**-0.5, accum_out=mean_sq[:]
             )
-            rms = stage.tile([P, 1], F32, tag="rms")
-            nc.scalar.activation(out=rms[:], in_=mean_sq[:], func=ACT.Sqrt, bias=eps[:])
+            shifted = stage.tile([P, 1], F32, tag="shifted")
+            nc.gpsimd.tensor_scalar(
+                out=shifted[:], in0=mean_sq[:], scalar1=1.0, scalar2=EPS, op0=ALU.mult, op1=ALU.add
+            )
             inv_rms[n] = stage.tile([P, 1], F32, tag="inv_rms", name="inv_rms%d" % n)
-            nc.vector.reciprocal(out=inv_rms[n][:], in_=rms[:])
+            nc.gpsimd.tensor_tensor(out=inv_rms[n][:], in0=shifted[:], in1=minus_half[:], op=ALU.pow)
 
         def norm(n):
             normed[n] = stage.tile([P, PAIR, H // PAIR], BF16, tag="normed", name="normed%d" % n)
@@ -187,7 +190,7 @@ def tile_memresprojections_pa_kernel(
                         nc.tensor.transpose(bank[:, g, u, :], words[:, first : first + P], ident_f32[:])
                 row_banks.append(bank)
             for j in range(ROW_BLOCKS):
-                copy = nc.vector.tensor_copy if j == ROW_BLOCKS - 1 else nc.scalar.copy
+                copy = nc.vector.tensor_copy if j == 0 else nc.scalar.copy
                 copy(
                     out=as_words[:, :, j * P : (j + 1) * P, :],
                     in_=row_banks[j][:].rearrange("p g u r -> p g r u"),
@@ -203,18 +206,17 @@ def tile_memresprojections_pa_kernel(
                 )
             return codes, scales
 
-        mean_square(0)
-        norm(0)
-        q_mx = [quantise_rows(q_rows0, "q0")]
-        turn(0)
-        group(0)
-        quantise(0)
-        mean_square(1)
-        norm(1)
-        q_mx.append(quantise_rows(q_rows1, "q1"))
-        mean_square(2)
-        norm(2)
+        for n in range(NORM_AHEAD):
+            mean_square(n)
+            norm(n)
+        for n in range(TURN_AHEAD):
+            turn(n)
+            group(n)
+            quantise(n)
+        q_mx = [quantise_rows(q_rows0, "q0"), quantise_rows(q_rows1, "q1")]
         k_mx = [quantise_rows(k_rows0, "k0"), quantise_rows(k_rows1, "k1")]
+        for n in range(NORM_AHEAD, SQUARE_AHEAD):
+            mean_square(n)
 
         q_copies = [nc.scalar.copy, nc.vector.tensor_copy]
         k_copies = [nc.vector.tensor_copy, nc.vector.tensor_copy]
@@ -234,8 +236,9 @@ def tile_memresprojections_pa_kernel(
             if n + TURN_AHEAD < TILES:
                 quantise(n + TURN_AHEAD)
             store(k_sums, k_copies, out_1[b, i * P : (i + 1) * P, :])
+            if n + SQUARE_AHEAD < TILES:
+                mean_square(n + SQUARE_AHEAD)
             if n + NORM_AHEAD < TILES:
-                mean_square(n + NORM_AHEAD)
                 norm(n + NORM_AHEAD)
             if n == 0:
                 memory_mx = quantise_rows(memory_rows, "memory")

from contextlib import ExitStack

import concourse.masks as masks
import concourse.mybir as mybir

F32 = mybir.dt.float32
BF16 = mybir.dt.bfloat16
I32 = mybir.dt.int32
U32 = mybir.dt.uint32
U8 = mybir.dt.uint8
FP8X4 = mybir.dt.float8_e4m3fn_x4
ACT = mybir.ActivationFunctionType
ALU = mybir.AluOpType

P = 128
PACK = 4
PAIR = 2
BATCHES, TOKENS, MEMORY, H, D = 4, 384, 128, 1024, 1024
EPS = 1e-6
PASSES = H // (P * PACK)
HALVES = PACK // PAIR
BATCH_TILES = TOKENS // P
TILES = BATCHES * BATCH_TILES
N_TILE = 512
ROW_BLOCKS = N_TILE // P
COLUMN_TILES = D // N_TILE
SQUARE_AHEAD = 4
NORM_AHEAD = 3
TURN_AHEAD = 1

FLOPS = 2 * H * D * BATCHES * (TOKENS + TOKENS + MEMORY)


def tile_memresprojections_pa_kernel(
    tc, hidden_states, memory_state, q_w, k_w, norm_w, out_0, out_1
):
    nc = tc.nc
    with ExitStack() as ctx:
        ctx.enter_context(tc.manual_schedule())
        const = ctx.enter_context(tc.tile_pool(name="const", bufs=1))
        inputs = ctx.enter_context(tc.tile_pool(name="inputs", bufs=1))
        operands = ctx.enter_context(tc.tile_pool(name="operands", bufs=1))
        stage = ctx.enter_context(tc.tile_pool(name="stage", bufs=4))
        results = ctx.enter_context(tc.tile_pool(name="results", bufs=8))
        banks = ctx.enter_context(tc.psum_pool(name="banks", bufs=8))

        gain_row = const.tile([P, H], BF16)
        nc.vector.memset(gain_row[:].bitcast(I32), 0)
        nc.sync.dma_start(out=gain_row[0:1, :], in_=norm_w.unsqueeze(0))

        token_rows = hidden_states.flatten_outer_dims()
        tokens = {}

        def load_tokens(n):
            tokens[n] = inputs.tile([P, H], BF16, name="tokens%d" % n)
            nc.sync.dma_start(out=tokens[n][:], in_=token_rows[n * P : (n + 1) * P, :])

        def load_rows(source, label):
            rows = inputs.tile([P, ROW_BLOCKS, H], BF16, name=label)
            nc.sync.dma_start(out=rows[:], in_=source.rearrange("(j p) h -> p j h", p=P))
            return rows

        for n in range(NORM_AHEAD):
            load_tokens(n)
        q_rows0 = load_rows(q_w[0:N_TILE, :], "q_rows0")
        q_rows1 = load_rows(q_w[N_TILE:D, :], "q_rows1")
        k_rows0 = load_rows(k_w[0:N_TILE, :], "k_rows0")
        k_rows1 = load_rows(k_w[N_TILE:D, :], "k_rows1")
        load_tokens(NORM_AHEAD)
        memory_rows = load_rows(memory_state.flatten_outer_dims(), "memory_rows")
        for n in range(NORM_AHEAD + 1, TILES):
            load_tokens(n)

        minus_half = const.tile([P, 1], F32)
        nc.vector.memset(minus_half[:], -0.5)
        table_warmer = const.tile([P, 1], F32)
        nc.scalar.activation(out=table_warmer[:], in_=minus_half[:], func=ACT.Square)
        ones = const.tile([P, P], BF16)
        nc.vector.memset(ones[:], 1.0)
        ident_f32 = const.tile([P, P], F32)
        masks.make_identity(nc, ident_f32[:])
        ident_bf16 = const.tile([P, P], BF16)
        masks.make_identity(nc, ident_bf16[:])

        gain = const.tile([P, PAIR, H // PAIR], BF16)
        pairs = N_TILE // PAIR
        for c in range(H // N_TILE):
            spread = banks.tile([P, N_TILE], F32, tag="bank")
            nc.tensor.matmul(
                spread[:], lhsT=ones[:], rhs=gain_row[:, c * N_TILE : (c + 1) * N_TILE],
                start=True, stop=True,
            )
            nc.vector.tensor_copy(
                out=gain[:, :, c * pairs : (c + 1) * pairs],
                in_=spread[:].rearrange("p (w e) -> p e w", e=PAIR),
            )

        inv_rms = {}
        normed = {}
        turned = {}
        grouped = {}
        pool_mx = {}

        def mean_square(n):
            squares = stage.tile([P, H], BF16, tag="squares")
            mean_sq = stage.tile([P, 1], F32, tag="mean_sq")
            nc.scalar.activation(
                out=squares[:], in_=tokens[n][:], func=ACT.Square, scale=H**-0.5, accum_out=mean_sq[:]
            )
            shifted = stage.tile([P, 1], F32, tag="shifted")
            nc.gpsimd.tensor_scalar(
                out=shifted[:], in0=mean_sq[:], scalar1=1.0, scalar2=EPS, op0=ALU.mult, op1=ALU.add
            )
            inv_rms[n] = stage.tile([P, 1], F32, tag="inv_rms", name="inv_rms%d" % n)
            nc.gpsimd.tensor_tensor(out=inv_rms[n][:], in0=shifted[:], in1=minus_half[:], op=ALU.pow)

        def norm(n):
            normed[n] = stage.tile([P, PAIR, H // PAIR], BF16, tag="normed", name="normed%d" % n)
            nc.vector.scalar_tensor_tensor(
                out=normed[n][:],
                in0=tokens[n][:].rearrange("p (w e) -> p e w", e=PAIR),
                scalar=inv_rms[n][:],
                in1=gain[:],
                op0=ALU.mult,
                op1=ALU.mult,
            )

        def turn(n):
            turned[n] = banks.tile([P, PASSES, PACK, P], BF16, tag="bank", name="turned%d" % n)
            for g in range(PASSES):
                for u in range(HALVES):
                    first = (HALVES * g + u) * P
                    for e in range(PAIR):
                        nc.tensor.transpose(
                            turned[n][:, g, PAIR * u + e, :], normed[n][:, e, first : first + P], ident_bf16[:]
                        )

        def group(n):
            grouped[n] = stage.tile(
                [P, PASSES, P, PACK], BF16, tag="grouped", name="grouped%d" % n, align_bytes=64
            )
            nc.scalar.copy(out=grouped[n][:], in_=turned[n][:].rearrange("p g t r -> p g r t"))

        def quantise(n):
            codes = operands.tile([P, PASSES, P], U32, name="codes%d" % n, align_bytes=64)
            scales = operands.tile([P, PASSES, P], U8, name="scales%d" % n, align_bytes=64)
            nc.vector.quantize_mx(
                out=codes[:].rearrange("p g r -> p (g r)").bitcast(FP8X4),
                scales=scales[:].rearrange("p g r -> p (g r)"),
                in_=grouped[n][:].rearrange("p g r t -> p (g r t)"),
            )
            pool_mx[n] = (codes, scales)

        def matmuls(token_mx, token_columns, weight_mx):
            token_codes, token_scales = token_mx
            sums = []
            for weight_codes, weight_scales in weight_mx:
                bank = banks.tile([P, N_TILE], F32, tag="bank")
                for g in range(PASSES):
                    nc.tensor.matmul_mx(
                        out=bank[:],
                        lhsT=token_codes[:, g, token_columns].bitcast(FP8X4),
                        lhsT_scale=token_scales[:, g, token_columns],
                        rhs=weight_codes[:, g, :].bitcast(FP8X4),
                        rhs_scale=weight_scales[:, g, :],
                        start=(g == 0),
                        stop=(g == PASSES - 1),
                    )
                sums.append(bank)
            return sums

        def store(sums, copies, out_rows):
            result = results.tile([P, D], F32, tag="result")
            for c in range(COLUMN_TILES):
                copies[c](out=result[:, c * N_TILE : (c + 1) * N_TILE], in_=sums[c][:])
            nc.sync.dma_start(out=out_rows, in_=result[:])

        def quantise_rows(rows, label):
            side_by_side = stage.tile(
                [P, PASSES * N_TILE * PACK], BF16, tag="side_by_side", bufs=2, align_bytes=64
            )
            as_words = side_by_side[:].bitcast(F32).rearrange("p (g r u) -> p g r u", g=PASSES, u=HALVES)
            row_banks = []
            for j in range(ROW_BLOCKS):
                words = rows[:, j, :].bitcast(F32)
                bank = banks.tile([P, PASSES, HALVES, P], F32, tag="bank")
                for g in range(PASSES):
                    for u in range(HALVES):
                        first = (HALVES * g + u) * P
                        nc.tensor.transpose(bank[:, g, u, :], words[:, first : first + P], ident_f32[:])
                row_banks.append(bank)
            for j in range(ROW_BLOCKS):
                copy = nc.vector.tensor_copy if j == 0 else nc.scalar.copy
                copy(
                    out=as_words[:, :, j * P : (j + 1) * P, :],
                    in_=row_banks[j][:].rearrange("p g u r -> p g r u"),
                )
            codes = operands.tile([P, PASSES, N_TILE], U32, name=label + "_codes", align_bytes=64)
            scales = operands.tile([P, PASSES, N_TILE], U8, name=label + "_scales", align_bytes=64)
            width = N_TILE * PACK
            for g in range(PASSES):
                nc.vector.quantize_mx(
                    out=codes[:, g, :].bitcast(FP8X4),
                    scales=scales[:, g, :],
                    in_=side_by_side[:, g * width : (g + 1) * width],
                )
            return codes, scales

        for n in range(NORM_AHEAD):
            mean_square(n)
            norm(n)
        for n in range(TURN_AHEAD):
            turn(n)
            group(n)
            quantise(n)
        q_mx = [quantise_rows(q_rows0, "q0"), quantise_rows(q_rows1, "q1")]
        k_mx = [quantise_rows(k_rows0, "k0"), quantise_rows(k_rows1, "k1")]
        for n in range(NORM_AHEAD, SQUARE_AHEAD):
            mean_square(n)

        q_copies = [nc.scalar.copy, nc.vector.tensor_copy]
        k_copies = [nc.vector.tensor_copy, nc.vector.tensor_copy]
        memory_copies = [nc.scalar.copy, nc.scalar.copy]

        q_out = out_0.flatten_outer_dims()
        all_columns = slice(0, P)
        for n in range(TILES):
            b, i = divmod(n, BATCH_TILES)
            if n + TURN_AHEAD < TILES:
                turn(n + TURN_AHEAD)
            q_sums = matmuls(pool_mx[n], all_columns, q_mx)
            k_sums = matmuls(pool_mx[n], all_columns, k_mx)
            if n + TURN_AHEAD < TILES:
                group(n + TURN_AHEAD)
            store(q_sums, q_copies, q_out[n * P : (n + 1) * P, :])
            if n + TURN_AHEAD < TILES:
                quantise(n + TURN_AHEAD)
            store(k_sums, k_copies, out_1[b, i * P : (i + 1) * P, :])
            if n + SQUARE_AHEAD < TILES:
                mean_square(n + SQUARE_AHEAD)
            if n + NORM_AHEAD < TILES:
                norm(n + NORM_AHEAD)
            if n == 0:
                memory_mx = quantise_rows(memory_rows, "memory")
            if i == BATCH_TILES - 1:
                memory_sums = matmuls(memory_mx, slice(b * P, (b + 1) * P), k_mx)
                store(memory_sums, memory_copies, out_1[b, TOKENS : TOKENS + MEMORY, :])
